import numpy as np
import ml_dtypes


def mxq(x, axis, fmt="e4m3"):
    dtype, down = {"e4m3": (ml_dtypes.float8_e4m3fn, 7), "e5m2": (ml_dtypes.float8_e5m2, 14)}[fmt]
    v = np.moveaxis(np.asarray(x, np.float32).astype(ml_dtypes.bfloat16).astype(np.float64), axis, -1)
    blocks = v.reshape(v.shape[:-1] + (-1, 32))
    amax = np.abs(blocks).max(-1, keepdims=True)
    byte = np.maximum(np.where(amax > 0, np.frexp(amax)[1] - 1 + 127, 0) - down, 1)
    scale = np.exp2(byte - 127.0)
    codes = (blocks / scale).astype(np.float32).astype(dtype).astype(np.float64)
    return np.moveaxis((codes * scale).reshape(v.shape), -1, axis)


WIDE = False


def mx_kscale(k):
    if not WIDE:
        return np.ones(k)
    levels = np.array([20, -20, 10, -10, 0])
    a = np.random.permutation(np.resize(levels, k // 512 * 4)).reshape(k // 512, 4)
    idx = np.arange(k)
    return np.exp2(a[idx // 512, idx % 128 // 32])


BF16 = ml_dtypes.bfloat16


def bf(x):
    return np.asarray(x, np.float32).astype(BF16)


def f64(x):
    return np.asarray(x).astype(np.float64)


N, IN, OUT = 3072, 1152, 1024
GROUP_MANTISSA = 8
GROUP_SIZE = 36


def bfp_quantize(x, mantissa=GROUP_MANTISSA, group_size=GROUP_SIZE):
    flat = x.reshape(-1)
    g = flat.reshape(-1, group_size)
    absmax = np.max(np.abs(g), axis=1, keepdims=True)
    e = np.floor(np.log2(np.where(absmax > 0, absmax, 1.0)))
    step = np.exp2(e - (mantissa - 1))
    q = np.trunc(g / step) * step
    q = np.where(absmax > 0, q, g)
    return q.reshape(x.shape)


def on_grid(x):
    return bf(bfp_quantize(f64(bf(x))))


def setup_inputs():
    u = mx_kscale(OUT)
    x = np.random.standard_normal((N, IN))
    w = np.random.uniform(-1.0, 1.0, (OUT, IN)) * 3.0 / np.sqrt(IN) / u[:, None]
    b = np.random.uniform(-0.5, 0.5, OUT)
    g = np.random.standard_normal((N, OUT)) * np.exp2(np.random.randint(-12, 1, (N, 1))) * 16.0 * u
    return {"input": on_grid(x), "weight": on_grid(w), "bias": bf(b), "grad_out": bf(g)}


def reference(input, weight, bias, grad_out):
    return mxq(f64(grad_out), 1, "e5m2") @ mxq(f64(weight), 0, "e4m3")

@@ -1,0 +1,191 @@
+from contextlib import ExitStack
+
+import concourse.mybir as mybir
+from concourse.masks import make_identity
+
+BF16 = mybir.dt.bfloat16
+F32 = mybir.dt.float32
+U32 = mybir.dt.uint32
+U8 = mybir.dt.uint8
+E4M3_X4 = mybir.dt.float8_e4m3fn_x4
+E5M2_X4 = mybir.dt.float8_e5m2_x4
+
+TOKENS = 3072
+K = 1024
+COLS = 1152
+
+P = 128
+PACK = 4
+K_PASS = P * PACK
+PASSES = K // K_PASS
+HALF = K_PASS // 2
+N_MOVE = 512
+
+SUB = 4
+GROUP = P * SUB
+GROUPS = TOKENS // GROUP
+WIDE = (COLS // N_MOVE) * N_MOVE
+WINDOWS = WIDE // N_MOVE
+REST = COLS - WIDE
+
+FLOPS = 2 * TOKENS * K * COLS
+BYTES = TOKENS * K * 2 + K * COLS * 2 + TOKENS * COLS * 4
+
+
+def tile_bflinear_t_kernel(tc, x_in, weight, bias, grad_out, out):
+    nc = tc.nc
+    g_dram = grad_out.rearrange("(s p j) k -> s p (j k)", p=P, j=SUB)
+    out_dram = out.rearrange("(s p j) n -> s p j n", p=P, j=SUB)
+
+    with ExitStack() as ctx:
+        keep = ctx.enter_context(tc.tile_pool(name="keep", bufs=1))
+        g_pool = ctx.enter_context(tc.tile_pool(name="g_pool", bufs=GROUPS))
+        q_pool = ctx.enter_context(tc.tile_pool(name="q_pool", bufs=2))
+        o_pool = ctx.enter_context(tc.tile_pool(name="o_pool", bufs=3))
+        t_psum = ctx.enter_context(tc.psum_pool(name="t_psum", bufs=4))
+        a_psum = ctx.enter_context(tc.psum_pool(name="a_psum", bufs=4))
+        ctx.enter_context(tc.manual_schedule())
+
+        g_raw = []
+        for s in range(GROUPS):
+            g_raw.append(g_pool.tile([P, SUB * K], BF16, name="g_raw"))
+        w_raw = keep.tile([P, PASSES, PACK, COLS], BF16)
+
+        nc.sync.dma_start(out=g_raw[0][:], in_=g_dram[0])
+        for c in range(PASSES):
+            for u in range(2):
+                k0 = c * K_PASS + u * HALF
+                nc.sync.dma_start(
+                    out=w_raw[:, c, 2 * u : 2 * u + 2, :],
+                    in_=weight[k0 : k0 + HALF, :].rearrange("(q e) n -> q e n", e=2),
+                )
+        for s in range(1, GROUPS):
+            nc.sync.dma_start(out=g_raw[s][:], in_=g_dram[s])
+
+        ident = keep.tile([P, P], F32)
+        make_identity(nc, ident[:])
+
+        w_grouped = keep.tile([P, PASSES, COLS, PACK], BF16, align_bytes=64)
+        w_codes = keep.tile([P, PASSES, COLS], U32, align_bytes=64)
+        w_scales = keep.tile([P, PASSES, COLS], U8, align_bytes=64)
+
+        g_codes = {}
+        g_scales = {}
+        g_grouped = {}
+        rest_sb = {}
+        out_sb = {}
+
+        def transpose_group(s):
+            words = g_raw[s][:].bitcast(F32).rearrange("p (j w) -> p j w", j=SUB)
+            g_grouped[s] = q_pool.tile([P, PASSES * GROUP * PACK], BF16, name="g_grouped", align_bytes=64)
+            banks = []
+            for c in range(PASSES):
+                for pair in range(SUB // 2):
+                    bank = t_psum.tile([P, 2, 2 * P], F32, name="t_bank")
+                    for u in range(2):
+                        for jj in range(2):
+                            w0 = (c * K_PASS + u * HALF) // 2
+                            nc.tensor.transpose(
+                                bank[:, u, jj * P : (jj + 1) * P],
+                                words[:, 2 * pair + jj, w0 : w0 + P],
+                                ident[:],
+                            )
+                    banks.append(bank)
+            return banks
+
+        def regroup_group(s, banks):
+            grouped_words = g_grouped[s][:].bitcast(F32).rearrange("p (c r u) -> p c r u", c=PASSES, u=2)
+            for c in range(PASSES):
+                for pair in range(SUB // 2):
+                    nc.vector.tensor_copy(
+                        out=grouped_words[:, c, 2 * pair * P : (2 * pair + 2) * P, :],
+                        in_=banks[c * (SUB // 2) + pair][:].rearrange("p u r -> p r u"),
+                    )
+
+        def quantise_group(s):
+            g_codes[s] = q_pool.tile([P, PASSES, GROUP], U32, name="g_codes", align_bytes=64)
+            g_scales[s] = q_pool.tile([P, PASSES, GROUP], U8, name="g_scales", align_bytes=64)
+            nc.vector.quantize_mx(
+                out=g_codes[s][:].rearrange("p c r -> p (c r)").bitcast(E5M2_X4),
+                scales=g_scales[s][:].rearrange("p c r -> p (c r)"),
+                in_=g_grouped[s][:],
+            )
+
+        def regroup_weight(c):
+            half = COLS // 2
+            for engine_copy, lo in ((nc.vector.tensor_copy, 0), (nc.scalar.copy, half)):
+                engine_copy(
+                    out=w_grouped[:, c, lo : lo + half, :].rearrange("p (n i) t -> p n t i", i=4),
+                    in_=w_raw[:, c, :, lo : lo + half].rearrange("p t (n i) -> p n t i", i=4),
+                )
+
+        def quantise_weight(c):
+            for lo, hi in ((0, WIDE), (WIDE, COLS)):
+                nc.vector.quantize_mx(
+                    out=w_codes[:, c, lo:hi].bitcast(E4M3_X4),
+                    scales=w_scales[:, c, lo:hi],
+                    in_=w_grouped[:, c, lo:hi, :].rearrange("p n t -> p (n t)"),
+                )
+
+        def rest_product(s):
+            acc = a_psum.tile([P, N_MOVE], F32, name="acc")
+            for c in range(PASSES):
+                nc.tensor.matmul_mx(
+                    out=acc[:],
+                    lhsT=w_codes[:, c, WIDE:COLS].bitcast(E4M3_X4),
+                    lhsT_scale=w_scales[:, c, WIDE:COLS],
+                    rhs=g_codes[s][:, c, :].bitcast(E5M2_X4),
+                    rhs_scale=g_scales[s][:, c, :],
+                    start=(c == 0),
+                    stop=(c == PASSES - 1),
+                )
+            rest_sb[s] = q_pool.tile([P, GROUP], F32, name="rest_sb")
+            nc.vector.tensor_copy(out=rest_sb[s][:], in_=acc[:])
+
+        def rest_transposes(s):
+            bank = a_psum.tile([P, SUB, P], F32, name="acc")
+            for j in range(SUB):
+                nc.tensor.transpose(bank[:, j, :], rest_sb[s][:, j * P : (j + 1) * P], ident[:])
+            return bank
+
+        def wide_product(s):
+            for j in range(SUB):
+                for n in range(WINDOWS):
+                    acc = a_psum.tile([P, N_MOVE], F32, name="acc")
+                    for c in range(PASSES):
+                        nc.tensor.matmul_mx(
+                            out=acc[:],
+                            lhsT=g_codes[s][:, c, j * P : (j + 1) * P].bitcast(E5M2_X4),
+                            lhsT_scale=g_scales[s][:, c, j * P : (j + 1) * P],
+                            rhs=w_codes[:, c, n * N_MOVE : (n + 1) * N_MOVE].bitcast(E4M3_X4),
+                            rhs_scale=w_scales[:, c, n * N_MOVE : (n + 1) * N_MOVE],
+                            start=(c == 0),
+                            stop=(c == PASSES - 1),
+                        )
+                    nc.scalar.copy(out=out_sb[s][:, j, n * N_MOVE : (n + 1) * N_MOVE], in_=acc[:])
+                if j % 2 == 1:
+                    nc.sync.dma_start(out=out_dram[s][:, j - 1 : j + 1, :], in_=out_sb[s][:, j - 1 : j + 1, :])
+
+        banks = transpose_group(0)
+        regroup_group(0, banks)
+        regroup_weight(0)
+        quantise_group(0)
+        quantise_weight(0)
+        regroup_weight(1)
+        quantise_weight(1)
+        rest_product(0)
+
+        for s in range(GROUPS):
+            more = s + 1 < GROUPS
+            if more:
+                banks = transpose_group(s + 1)
+            rest_bank = rest_transposes(s)
+            if more:
+                regroup_group(s + 1, banks)
+            out_sb[s] = o_pool.tile([P, SUB, COLS], F32, name="out_sb")
+            nc.vector.tensor_copy(out=out_sb[s][:, :, WIDE:COLS], in_=rest_bank[:])
+            if more:
+                quantise_group(s + 1)
+            wide_product(s)
+            if more:
+                rest_product(s + 1)

@@ -22,11 +22,13 @@ HALF = K_PASS // 2
 N_MOVE = 512
 
 SUB = 4
+PAIRS = SUB // 2
 GROUP = P * SUB
 GROUPS = TOKENS // GROUP
-WIDE = (COLS // N_MOVE) * N_MOVE
-WINDOWS = WIDE // N_MOVE
-REST = COLS - WIDE
+
+REST = (0, P)
+FIRST = (P, P + N_MOVE)
+SECOND = (P + N_MOVE, COLS)
 
 FLOPS = 2 * TOKENS * K * COLS
 BYTES = TOKENS * K * 2 + K * COLS * 2 + TOKENS * COLS * 4
@@ -40,8 +42,8 @@ def tile_bflinear_t_kernel(tc, x_in, weight, bias, grad_out, out):
     with ExitStack() as ctx:
         keep = ctx.enter_context(tc.tile_pool(name="keep", bufs=1))
         g_pool = ctx.enter_context(tc.tile_pool(name="g_pool", bufs=GROUPS))
-        q_pool = ctx.enter_context(tc.tile_pool(name="q_pool", bufs=2))
-        o_pool = ctx.enter_context(tc.tile_pool(name="o_pool", bufs=3))
+        two = ctx.enter_context(tc.tile_pool(name="two", bufs=2))
+        three = ctx.enter_context(tc.tile_pool(name="three", bufs=3))
         t_psum = ctx.enter_context(tc.psum_pool(name="t_psum", bufs=4))
         a_psum = ctx.enter_context(tc.psum_pool(name="a_psum", bufs=4))
         ctx.enter_context(tc.manual_schedule())
@@ -49,82 +51,82 @@ def tile_bflinear_t_kernel(tc, x_in, weight, bias, grad_out, out):
         g_raw = []
         for s in range(GROUPS):
             g_raw.append(g_pool.tile([P, SUB * K], BF16, name="g_raw"))
-        w_raw = keep.tile([P, PASSES, PACK, COLS], BF16)
-
-        nc.sync.dma_start(out=g_raw[0][:], in_=g_dram[0])
-        for c in range(PASSES):
-            for u in range(2):
-                k0 = c * K_PASS + u * HALF
-                nc.sync.dma_start(
-                    out=w_raw[:, c, 2 * u : 2 * u + 2, :],
-                    in_=weight[k0 : k0 + HALF, :].rearrange("(q e) n -> q e n", e=2),
-                )
-        for s in range(1, GROUPS):
-            nc.sync.dma_start(out=g_raw[s][:], in_=g_dram[s])
-
+        w_early = keep.tile([P, PASSES, PACK, FIRST[1]], BF16)
+        w_late = keep.tile([P, PASSES, PACK, N_MOVE], BF16)
+        w_raw = {REST: w_early[:, :, :, REST[0] : REST[1]], FIRST: w_early[:, :, :, FIRST[0] : FIRST[1]], SECOND: w_late[:]}
+        w_grouped = {}
+        w_codes = {}
+        w_scales = {}
+        for cols in (REST, FIRST, SECOND):
+            width = cols[1] - cols[0]
+            w_grouped[cols] = keep.tile([P, PASSES, width, PACK], BF16, name="w_grouped%d" % cols[0], align_bytes=64)
+            w_codes[cols] = keep.tile([P, PASSES, width], U32, name="w_codes%d" % cols[0], align_bytes=64)
+            w_scales[cols] = keep.tile([P, PASSES, width], U8, name="w_scales%d" % cols[0], align_bytes=64)
         ident = keep.tile([P, P], F32)
-        make_identity(nc, ident[:])
 
-        w_grouped = keep.tile([P, PASSES, COLS, PACK], BF16, align_bytes=64)
-        w_codes = keep.tile([P, PASSES, COLS], U32, align_bytes=64)
-        w_scales = keep.tile([P, PASSES, COLS], U8, align_bytes=64)
-
+        g_grouped = {}
         g_codes = {}
         g_scales = {}
-        g_grouped = {}
         rest_sb = {}
-        out_sb = {}
+        out_early = {}
+        out_late = {}
 
-        def transpose_group(s):
-            words = g_raw[s][:].bitcast(F32).rearrange("p (j w) -> p j w", j=SUB)
-            g_grouped[s] = q_pool.tile([P, PASSES * GROUP * PACK], BF16, name="g_grouped", align_bytes=64)
-            banks = []
+        def load_weight(tile_ap, lo, hi):
             for c in range(PASSES):
-                for pair in range(SUB // 2):
-                    bank = t_psum.tile([P, 2, 2 * P], F32, name="t_bank")
-                    for u in range(2):
-                        for jj in range(2):
-                            w0 = (c * K_PASS + u * HALF) // 2
-                            nc.tensor.transpose(
-                                bank[:, u, jj * P : (jj + 1) * P],
-                                words[:, 2 * pair + jj, w0 : w0 + P],
-                                ident[:],
-                            )
-                    banks.append(bank)
-            return banks
-
-        def regroup_group(s, banks):
-            grouped_words = g_grouped[s][:].bitcast(F32).rearrange("p (c r u) -> p c r u", c=PASSES, u=2)
-            for c in range(PASSES):
-                for pair in range(SUB // 2):
-                    nc.vector.tensor_copy(
-                        out=grouped_words[:, c, 2 * pair * P : (2 * pair + 2) * P, :],
-                        in_=banks[c * (SUB // 2) + pair][:].rearrange("p u r -> p r u"),
+                for u in range(2):
+                    k0 = c * K_PASS + u * HALF
+                    nc.sync.dma_start(
+                        out=tile_ap[:, c, 2 * u : 2 * u + 2, :],
+                        in_=weight[k0 : k0 + HALF, lo:hi].rearrange("(q e) n -> q e n", e=2),
                     )
 
-        def quantise_group(s):
-            g_codes[s] = q_pool.tile([P, PASSES, GROUP], U32, name="g_codes", align_bytes=64)
-            g_scales[s] = q_pool.tile([P, PASSES, GROUP], U8, name="g_scales", align_bytes=64)
-            nc.vector.quantize_mx(
-                out=g_codes[s][:].rearrange("p c r -> p (c r)").bitcast(E5M2_X4),
-                scales=g_scales[s][:].rearrange("p c r -> p (c r)"),
-                in_=g_grouped[s][:],
-            )
-
-        def regroup_weight(c):
-            half = COLS // 2
-            for engine_copy, lo in ((nc.vector.tensor_copy, 0), (nc.scalar.copy, half)):
+        def regroup_weight(c, cols):
+            width = cols[1] - cols[0]
+            cut = width * 5 // 8
+            for engine_copy, a, b in ((nc.vector.tensor_copy, 0, cut), (nc.scalar.copy, cut, width)):
                 engine_copy(
-                    out=w_grouped[:, c, lo : lo + half, :].rearrange("p (n i) t -> p n t i", i=4),
-                    in_=w_raw[:, c, :, lo : lo + half].rearrange("p t (n i) -> p n t i", i=4),
+                    out=w_grouped[cols][:, c, a:b, :].rearrange("p (n i) t -> p n t i", i=4),
+                    in_=w_raw[cols][:, c, :, a:b].rearrange("p t (n i) -> p n t i", i=4),
                 )
 
-        def quantise_weight(c):
-            for lo, hi in ((0, WIDE), (WIDE, COLS)):
+        def quantise_weight(c, cols):
+            nc.vector.quantize_mx(
+                out=w_codes[cols][:, c, :].bitcast(E4M3_X4),
+                scales=w_scales[cols][:, c, :],
+                in_=w_grouped[cols][:, c, :, :].rearrange("p n t -> p (n t)"),
+            )
+
+        def transpose_pair(s, pair):
+            if pair == 0:
+                g_grouped[s] = two.tile([P, PASSES * GROUP * PACK], BF16, name="g_grouped", align_bytes=64)
+            words = g_raw[s][:].bitcast(F32).rearrange("p (j w) -> p j w", j=SUB)
+            grouped_words = g_grouped[s][:].bitcast(F32).rearrange("p (c r u) -> p c r u", c=PASSES, u=2)
+            for c in range(PASSES):
+                bank = t_psum.tile([P, 2, 2 * P], F32, name="t_bank")
+                for u in range(2):
+                    for jj in range(2):
+                        w0 = (c * K_PASS + u * HALF) // 2
+                        nc.tensor.transpose(
+                            bank[:, u, jj * P : (jj + 1) * P],
+                            words[:, 2 * pair + jj, w0 : w0 + P],
+                            ident[:],
+                        )
+                nc.scalar.copy(
+                    out=grouped_words[:, c, 2 * pair * P : (2 * pair + 2) * P, :],
+                    in_=bank[:].rearrange("p u r -> p r u"),
+                )
+
+        def quantise_pair(s, pair):
+            if pair == 0:
+                g_codes[s] = three.tile([P, PASSES, GROUP], U32, name="g_codes", align_bytes=64)
+                g_scales[s] = three.tile([P, PASSES, GROUP], U8, name="g_scales", align_bytes=64)
+            grouped = g_grouped[s][:].rearrange("p (c x) -> p c x", c=PASSES)
+            r0 = 2 * pair * P
+            for c in range(PASSES):
                 nc.vector.quantize_mx(
-                    out=w_codes[:, c, lo:hi].bitcast(E4M3_X4),
-                    scales=w_scales[:, c, lo:hi],
-                    in_=w_grouped[:, c, lo:hi, :].rearrange("p n t -> p (n t)"),
+                    out=g_codes[s][:, c, r0 : r0 + 2 * P].bitcast(E5M2_X4),
+                    scales=g_scales[s][:, c, r0 : r0 + 2 * P],
+                    in_=grouped[:, c, r0 * PACK : (r0 + 2 * P) * PACK],
                 )
 
         def rest_product(s):
@@ -132,60 +134,92 @@ def tile_bflinear_t_kernel(tc, x_in, weight, bias, grad_out, out):
             for c in range(PASSES):
                 nc.tensor.matmul_mx(
                     out=acc[:],
-                    lhsT=w_codes[:, c, WIDE:COLS].bitcast(E4M3_X4),
-                    lhsT_scale=w_scales[:, c, WIDE:COLS],
+                    lhsT=w_codes[REST][:, c, :].bitcast(E4M3_X4),
+                    lhsT_scale=w_scales[REST][:, c, :],
                     rhs=g_codes[s][:, c, :].bitcast(E5M2_X4),
                     rhs_scale=g_scales[s][:, c, :],
                     start=(c == 0),
                     stop=(c == PASSES - 1),
                 )
-            rest_sb[s] = q_pool.tile([P, GROUP], F32, name="rest_sb")
+            rest_sb[s] = two.tile([P, GROUP], F32, name="rest_sb")
             nc.vector.tensor_copy(out=rest_sb[s][:], in_=acc[:])
 
         def rest_transposes(s):
+            lo, hi = REST
             bank = a_psum.tile([P, SUB, P], F32, name="acc")
             for j in range(SUB):
                 nc.tensor.transpose(bank[:, j, :], rest_sb[s][:, j * P : (j + 1) * P], ident[:])
-            return bank
+            nc.vector.tensor_copy(out=out_early[s][:, :, lo:hi], in_=bank[:])
 
-        def wide_product(s):
-            for j in range(SUB):
-                for n in range(WINDOWS):
-                    acc = a_psum.tile([P, N_MOVE], F32, name="acc")
-                    for c in range(PASSES):
-                        nc.tensor.matmul_mx(
-                            out=acc[:],
-                            lhsT=g_codes[s][:, c, j * P : (j + 1) * P].bitcast(E5M2_X4),
-                            lhsT_scale=g_scales[s][:, c, j * P : (j + 1) * P],
-                            rhs=w_codes[:, c, n * N_MOVE : (n + 1) * N_MOVE].bitcast(E4M3_X4),
-                            rhs_scale=w_scales[:, c, n * N_MOVE : (n + 1) * N_MOVE],
-                            start=(c == 0),
-                            stop=(c == PASSES - 1),
-                        )
-                    nc.scalar.copy(out=out_sb[s][:, j, n * N_MOVE : (n + 1) * N_MOVE], in_=acc[:])
-                if j % 2 == 1:
-                    nc.sync.dma_start(out=out_dram[s][:, j - 1 : j + 1, :], in_=out_sb[s][:, j - 1 : j + 1, :])
+        def window_product(s, j, cols, dest):
+            acc = a_psum.tile([P, N_MOVE], F32, name="acc")
+            for c in range(PASSES):
+                nc.tensor.matmul_mx(
+                    out=acc[:],
+                    lhsT=g_codes[s][:, c, j * P : (j + 1) * P].bitcast(E5M2_X4),
+                    lhsT_scale=g_scales[s][:, c, j * P : (j + 1) * P],
+                    rhs=w_codes[cols][:, c, :].bitcast(E4M3_X4),
+                    rhs_scale=w_scales[cols][:, c, :],
+                    start=(c == 0),
+                    stop=(c == PASSES - 1),
+                )
+            if j % 2 == 0:
+                nc.vector.tensor_copy(out=dest, in_=acc[:])
+            else:
+                nc.scalar.copy(out=dest, in_=acc[:])
 
-        banks = transpose_group(0)
-        regroup_group(0, banks)
-        regroup_weight(0)
-        quantise_group(0)
-        quantise_weight(0)
-        regroup_weight(1)
-        quantise_weight(1)
-        rest_product(0)
+        def first_window(s, j):
+            window_product(s, j, FIRST, out_early[s][:, j, FIRST[0] : FIRST[1]])
 
-        for s in range(GROUPS):
-            more = s + 1 < GROUPS
-            if more:
-                banks = transpose_group(s + 1)
-            rest_bank = rest_transposes(s)
-            if more:
-                regroup_group(s + 1, banks)
-            out_sb[s] = o_pool.tile([P, SUB, COLS], F32, name="out_sb")
-            nc.vector.tensor_copy(out=out_sb[s][:, :, WIDE:COLS], in_=rest_bank[:])
-            if more:
-                quantise_group(s + 1)
-            wide_product(s)
-            if more:
-                rest_product(s + 1)
+        def second_window(s, j):
+            window_product(s, j, SECOND, out_late[s][:, j, :])
+            nc.sync.dma_start(out=out_dram[s][:, j, SECOND[0] : SECOND[1]], in_=out_late[s][:, j, :])
+
+        nc.sync.dma_start(out=g_raw[0][:, 0 : 2 * K], in_=g_dram[0][:, 0 : 2 * K])
+        load_weight(w_early, REST[0], FIRST[1])
+        nc.sync.dma_start(out=g_raw[0][:, 2 * K : 4 * K], in_=g_dram[0][:, 2 * K : 4 * K])
+        nc.sync.dma_start(out=g_raw[1][:], in_=g_dram[1])
+        load_weight(w_late, SECOND[0], SECOND[1])
+        for s in range(2, GROUPS):
+            nc.sync.dma_start(out=g_raw[s][:], in_=g_dram[s])
+
+        make_identity(nc, ident[:])
+
+        transpose_pair(0, 0)
+        regroup_weight(0, FIRST)
+        quantise_pair(0, 0)
+        regroup_weight(1, FIRST)
+        quantise_weight(0, FIRST)
+        quantise_weight(1, FIRST)
+        transpose_pair(0, 1)
+        regroup_weight(0, REST)
+        regroup_weight(1, REST)
+        quantise_pair(0, 1)
+        quantise_weight(0, REST)
+        quantise_weight(1, REST)
+
+        for s in range(GROUPS + 1):
+            if s < GROUPS:
+                out_early[s] = three.tile([P, SUB, FIRST[1]], F32, name="out_early")
+                first_window(s, 0)
+                first_window(s, 1)
+                rest_product(s)
+                if s + 1 < GROUPS:
+                    transpose_pair(s + 1, 0)
+                    transpose_pair(s + 1, 1)
+                rest_transposes(s)
+                first_window(s, 2)
+                first_window(s, 3)
+                nc.sync.dma_start(out=out_dram[s][:, :, 0 : FIRST[1]], in_=out_early[s][:])
+                if s + 1 < GROUPS:
+                    quantise_pair(s + 1, 0)
+                    quantise_pair(s + 1, 1)
+            if s == 0:
+                regroup_weight(0, SECOND)
+                regroup_weight(1, SECOND)
+                quantise_weight(0, SECOND)
+                quantise_weight(1, SECOND)
+            if s >= 1:
+                out_late[s - 1] = three.tile([P, SUB, N_MOVE], F32, name="out_late")
+                for j in range(SUB):
+                    second_window(s - 1, j)

@@ -26,9 +26,10 @@ PAIRS = SUB // 2
 GROUP = P * SUB
 GROUPS = TOKENS // GROUP
 
-REST = (0, P)
-FIRST = (P, P + N_MOVE)
-SECOND = (P + N_MOVE, COLS)
+FIRST = (0, N_MOVE)
+SECOND = (N_MOVE, 2 * N_MOVE)
+REST = (2 * N_MOVE, COLS)
+LATE = COLS - N_MOVE
 
 FLOPS = 2 * TOKENS * K * COLS
 BYTES = TOKENS * K * 2 + K * COLS * 2 + TOKENS * COLS * 4
@@ -44,21 +45,19 @@ def tile_bflinear_t_kernel(tc, x_in, weight, bias, grad_out, out):
         g_pool = ctx.enter_context(tc.tile_pool(name="g_pool", bufs=GROUPS))
         two = ctx.enter_context(tc.tile_pool(name="two", bufs=2))
         three = ctx.enter_context(tc.tile_pool(name="three", bufs=3))
-        t_psum = ctx.enter_context(tc.psum_pool(name="t_psum", bufs=4))
-        a_psum = ctx.enter_context(tc.psum_pool(name="a_psum", bufs=4))
+        psum = ctx.enter_context(tc.psum_pool(name="psum", bufs=8))
         ctx.enter_context(tc.manual_schedule())
 
         g_raw = []
         for s in range(GROUPS):
             g_raw.append(g_pool.tile([P, SUB * K], BF16, name="g_raw"))
-        w_early = keep.tile([P, PASSES, PACK, FIRST[1]], BF16)
-        w_late = keep.tile([P, PASSES, PACK, N_MOVE], BF16)
-        w_raw = {REST: w_early[:, :, :, REST[0] : REST[1]], FIRST: w_early[:, :, :, FIRST[0] : FIRST[1]], SECOND: w_late[:]}
+        w_raw = {}
         w_grouped = {}
         w_codes = {}
         w_scales = {}
-        for cols in (REST, FIRST, SECOND):
+        for cols in (FIRST, SECOND, REST):
             width = cols[1] - cols[0]
+            w_raw[cols] = keep.tile([P, PASSES, PACK, width], BF16, name="w_raw%d" % cols[0])
             w_grouped[cols] = keep.tile([P, PASSES, width, PACK], BF16, name="w_grouped%d" % cols[0], align_bytes=64)
             w_codes[cols] = keep.tile([P, PASSES, width], U32, name="w_codes%d" % cols[0], align_bytes=64)
             w_scales[cols] = keep.tile([P, PASSES, width], U8, name="w_scales%d" % cols[0], align_bytes=64)
@@ -71,13 +70,13 @@ def tile_bflinear_t_kernel(tc, x_in, weight, bias, grad_out, out):
         out_early = {}
         out_late = {}
 
-        def load_weight(tile_ap, lo, hi):
+        def load_weight(cols):
             for c in range(PASSES):
                 for u in range(2):
                     k0 = c * K_PASS + u * HALF
                     nc.sync.dma_start(
-                        out=tile_ap[:, c, 2 * u : 2 * u + 2, :],
-                        in_=weight[k0 : k0 + HALF, lo:hi].rearrange("(q e) n -> q e n", e=2),
+                        out=w_raw[cols][:, c, 2 * u : 2 * u + 2, :],
+                        in_=weight[k0 : k0 + HALF, cols[0] : cols[1]].rearrange("(q e) n -> q e n", e=2),
                     )
 
         def regroup_weight(c, cols):
@@ -96,13 +95,21 @@ def tile_bflinear_t_kernel(tc, x_in, weight, bias, grad_out, out):
                 in_=w_grouped[cols][:, c, :, :].rearrange("p n t -> p (n t)"),
             )
 
+        def prepare_weight(cols):
+            for c in range(PASSES):
+                regroup_weight(c, cols)
+            for c in range(PASSES):
+                quantise_weight(c, cols)
+
         def transpose_pair(s, pair):
             if pair == 0:
                 g_grouped[s] = two.tile([P, PASSES * GROUP * PACK], BF16, name="g_grouped", align_bytes=64)
+                g_codes[s] = three.tile([P, PASSES, GROUP], U32, name="g_codes", align_bytes=64)
+                g_scales[s] = three.tile([P, PASSES, GROUP], U8, name="g_scales", align_bytes=64)
             words = g_raw[s][:].bitcast(F32).rearrange("p (j w) -> p j w", j=SUB)
             grouped_words = g_grouped[s][:].bitcast(F32).rearrange("p (c r u) -> p c r u", c=PASSES, u=2)
             for c in range(PASSES):
-                bank = t_psum.tile([P, 2, 2 * P], F32, name="t_bank")
+                bank = psum.tile([P, 2, 2 * P], F32, name="bank")
                 for u in range(2):
                     for jj in range(2):
                         w0 = (c * K_PASS + u * HALF) // 2
@@ -116,24 +123,41 @@ def tile_bflinear_t_kernel(tc, x_in, weight, bias, grad_out, out):
                     in_=bank[:].rearrange("p u r -> p r u"),
                 )
 
-        def quantise_pair(s, pair):
-            if pair == 0:
-                g_codes[s] = three.tile([P, PASSES, GROUP], U32, name="g_codes", align_bytes=64)
-                g_scales[s] = three.tile([P, PASSES, GROUP], U8, name="g_scales", align_bytes=64)
+        def quantise_pair(s, pair, c):
             grouped = g_grouped[s][:].rearrange("p (c x) -> p c x", c=PASSES)
             r0 = 2 * pair * P
+            nc.vector.quantize_mx(
+                out=g_codes[s][:, c, r0 : r0 + 2 * P].bitcast(E5M2_X4),
+                scales=g_scales[s][:, c, r0 : r0 + 2 * P],
+                in_=grouped[:, c, r0 * PACK : (r0 + 2 * P) * PACK],
+            )
+
+        def window_pair(s, pair, cols, dest):
+            banks = [psum.tile([P, N_MOVE], F32, name="bank"), psum.tile([P, N_MOVE], F32, name="bank")]
             for c in range(PASSES):
-                nc.vector.quantize_mx(
-                    out=g_codes[s][:, c, r0 : r0 + 2 * P].bitcast(E5M2_X4),
-                    scales=g_scales[s][:, c, r0 : r0 + 2 * P],
-                    in_=grouped[:, c, r0 * PACK : (r0 + 2 * P) * PACK],
-                )
+                for jj in range(2):
+                    r0 = (2 * pair + jj) * P
+                    nc.tensor.matmul_mx(
+                        out=banks[jj][:],
+                        lhsT=g_codes[s][:, c, r0 : r0 + P].bitcast(E5M2_X4),
+                        lhsT_scale=g_scales[s][:, c, r0 : r0 + P],
+                        rhs=w_codes[cols][:, c, :].bitcast(E4M3_X4),
+                        rhs_scale=w_scales[cols][:, c, :],
+                        start=(c == 0),
+                        stop=(c == PASSES - 1),
+                    )
+            nc.vector.tensor_copy(out=dest[:, 2 * pair, 0:N_MOVE], in_=banks[0][:])
+            nc.scalar.copy(out=dest[:, 2 * pair + 1, 0:N_MOVE], in_=banks[1][:])
+
+        def store_early(s, pair):
+            j0 = 2 * pair
+            nc.sync.dma_start(out=out_dram[s][:, j0 : j0 + 2, FIRST[0] : FIRST[1]], in_=out_early[s][:, j0 : j0 + 2, :])
 
         def rest_product(s):
-            acc = a_psum.tile([P, N_MOVE], F32, name="acc")
+            bank = psum.tile([P, N_MOVE], F32, name="bank")
             for c in range(PASSES):
                 nc.tensor.matmul_mx(
-                    out=acc[:],
+                    out=bank[:],
                     lhsT=w_codes[REST][:, c, :].bitcast(E4M3_X4),
                     lhsT_scale=w_scales[REST][:, c, :],
                     rhs=g_codes[s][:, c, :].bitcast(E5M2_X4),
@@ -142,84 +166,63 @@ def tile_bflinear_t_kernel(tc, x_in, weight, bias, grad_out, out):
                     stop=(c == PASSES - 1),
                 )
             rest_sb[s] = two.tile([P, GROUP], F32, name="rest_sb")
-            nc.vector.tensor_copy(out=rest_sb[s][:], in_=acc[:])
+            nc.scalar.copy(out=rest_sb[s][:], in_=bank[:])
 
         def rest_transposes(s):
-            lo, hi = REST
-            bank = a_psum.tile([P, SUB, P], F32, name="acc")
+            bank = psum.tile([P, SUB, P], F32, name="bank")
             for j in range(SUB):
                 nc.tensor.transpose(bank[:, j, :], rest_sb[s][:, j * P : (j + 1) * P], ident[:])
-            nc.vector.tensor_copy(out=out_early[s][:, :, lo:hi], in_=bank[:])
-
-        def window_product(s, j, cols, dest):
-            acc = a_psum.tile([P, N_MOVE], F32, name="acc")
-            for c in range(PASSES):
-                nc.tensor.matmul_mx(
-                    out=acc[:],
-                    lhsT=g_codes[s][:, c, j * P : (j + 1) * P].bitcast(E5M2_X4),
-                    lhsT_scale=g_scales[s][:, c, j * P : (j + 1) * P],
-                    rhs=w_codes[cols][:, c, :].bitcast(E4M3_X4),
-                    rhs_scale=w_scales[cols][:, c, :],
-                    start=(c == 0),
-                    stop=(c == PASSES - 1),
-                )
-            if j % 2 == 0:
-                nc.vector.tensor_copy(out=dest, in_=acc[:])
-            else:
-                nc.scalar.copy(out=dest, in_=acc[:])
-
-        def first_window(s, j):
-            window_product(s, j, FIRST, out_early[s][:, j, FIRST[0] : FIRST[1]])
-
-        def second_window(s, j):
-            window_product(s, j, SECOND, out_late[s][:, j, :])
-            nc.sync.dma_start(out=out_dram[s][:, j, SECOND[0] : SECOND[1]], in_=out_late[s][:, j, :])
+            nc.vector.tensor_copy(out=out_late[s][:, :, N_MOVE:LATE], in_=bank[:])
 
         nc.sync.dma_start(out=g_raw[0][:, 0 : 2 * K], in_=g_dram[0][:, 0 : 2 * K])
-        load_weight(w_early, REST[0], FIRST[1])
+        load_weight(FIRST)
         nc.sync.dma_start(out=g_raw[0][:, 2 * K : 4 * K], in_=g_dram[0][:, 2 * K : 4 * K])
         nc.sync.dma_start(out=g_raw[1][:], in_=g_dram[1])
-        load_weight(w_late, SECOND[0], SECOND[1])
+        load_weight(REST)
+        load_weight(SECOND)
         for s in range(2, GROUPS):
             nc.sync.dma_start(out=g_raw[s][:], in_=g_dram[s])
 
         make_identity(nc, ident[:])
 
         transpose_pair(0, 0)
-        regroup_weight(0, FIRST)
-        quantise_pair(0, 0)
-        regroup_weight(1, FIRST)
-        quantise_weight(0, FIRST)
-        quantise_weight(1, FIRST)
+        for c in range(PASSES):
+            regroup_weight(c, FIRST)
+            quantise_pair(0, 0, c)
+            quantise_weight(c, FIRST)
         transpose_pair(0, 1)
-        regroup_weight(0, REST)
-        regroup_weight(1, REST)
-        quantise_pair(0, 1)
-        quantise_weight(0, REST)
-        quantise_weight(1, REST)
+        for c in range(PASSES):
+            quantise_pair(0, 1, c)
+        prepare_weight(REST)
 
         for s in range(GROUPS + 1):
-            if s < GROUPS:
-                out_early[s] = three.tile([P, SUB, FIRST[1]], F32, name="out_early")
-                first_window(s, 0)
-                first_window(s, 1)
-                rest_product(s)
-                if s + 1 < GROUPS:
-                    transpose_pair(s + 1, 0)
-                    transpose_pair(s + 1, 1)
-                rest_transposes(s)
-                first_window(s, 2)
-                first_window(s, 3)
-                nc.sync.dma_start(out=out_dram[s][:, :, 0 : FIRST[1]], in_=out_early[s][:])
-                if s + 1 < GROUPS:
-                    quantise_pair(s + 1, 0)
-                    quantise_pair(s + 1, 1)
+            now = s < GROUPS
+            ahead = s + 1 < GROUPS
+            behind = s >= 1
+            if now:
+                out_early[s] = three.tile([P, SUB, N_MOVE], F32, name="out_early")
+                window_pair(s, 0, FIRST, out_early[s])
+                store_early(s, 0)
+            if ahead:
+                transpose_pair(s + 1, 0)
+                transpose_pair(s + 1, 1)
+                for c in range(PASSES):
+                    quantise_pair(s + 1, 0, c)
+            if behind:
+                out_late[s - 1] = three.tile([P, SUB, LATE], F32, name="out_late")
+                rest_transposes(s - 1)
+            if now:
+                window_pair(s, 1, FIRST, out_early[s])
+                store_early(s, 1)
+            if ahead:
+                for c in range(PASSES):
+                    quantise_pair(s + 1, 1, c)
             if s == 0:
-                regroup_weight(0, SECOND)
-                regroup_weight(1, SECOND)
-                quantise_weight(0, SECOND)
-                quantise_weight(1, SECOND)
-            if s >= 1:
-                out_late[s - 1] = three.tile([P, SUB, N_MOVE], F32, name="out_late")
-                for j in range(SUB):
-                    second_window(s - 1, j)
+                prepare_weight(SECOND)
+            if now:
+                rest_product(s)
+            if behind:
+                for pair in range(PAIRS):
+                    window_pair(s - 1, pair, SECOND, out_late[s - 1])
+                    for j in (2 * pair, 2 * pair + 1):
+                        nc.sync.dma_start(out=out_dram[s - 1][:, j, SECOND[0] : REST[1]], in_=out_late[s - 1][:, j, :])

@@ -179,8 +179,9 @@ def tile_bflinear_t_kernel(tc, x_in, weight, bias, grad_out, out):
         nc.sync.dma_start(out=g_raw[0][:, 2 * K : 4 * K], in_=g_dram[0][:, 2 * K : 4 * K])
         nc.sync.dma_start(out=g_raw[1][:], in_=g_dram[1])
         load_weight(REST)
+        nc.sync.dma_start(out=g_raw[2][:], in_=g_dram[2])
         load_weight(SECOND)
-        for s in range(2, GROUPS):
+        for s in range(3, GROUPS):
             nc.sync.dma_start(out=g_raw[s][:], in_=g_dram[s])
 
         make_identity(nc, ident[:])
@@ -203,6 +204,8 @@ def tile_bflinear_t_kernel(tc, x_in, weight, bias, grad_out, out):
                 out_early[s] = three.tile([P, SUB, N_MOVE], F32, name="out_early")
                 window_pair(s, 0, FIRST, out_early[s])
                 store_early(s, 0)
+            if s == 1:
+                prepare_weight(SECOND)
             if ahead:
                 transpose_pair(s + 1, 0)
                 transpose_pair(s + 1, 1)
@@ -217,8 +220,6 @@ def tile_bflinear_t_kernel(tc, x_in, weight, bias, grad_out, out):
             if ahead:
                 for c in range(PASSES):
                     quantise_pair(s + 1, 1, c)
-            if s == 0:
-                prepare_weight(SECOND)
             if now:
                 rest_product(s)
             if behind:

@@ -29,7 +29,7 @@ GROUPS = TOKENS // GROUP
 FIRST = (0, N_MOVE)
 SECOND = (N_MOVE, 2 * N_MOVE)
 REST = (2 * N_MOVE, COLS)
-LATE = COLS - N_MOVE
+LAG = 2
 
 FLOPS = 2 * TOKENS * K * COLS
 BYTES = TOKENS * K * 2 + K * COLS * 2 + TOKENS * COLS * 4
@@ -42,7 +42,7 @@ def tile_bflinear_t_kernel(tc, x_in, weight, bias, grad_out, out):
 
     with ExitStack() as ctx:
         keep = ctx.enter_context(tc.tile_pool(name="keep", bufs=1))
-        g_pool = ctx.enter_context(tc.tile_pool(name="g_pool", bufs=GROUPS))
+        per_group = ctx.enter_context(tc.tile_pool(name="per_group", bufs=GROUPS))
         two = ctx.enter_context(tc.tile_pool(name="two", bufs=2))
         three = ctx.enter_context(tc.tile_pool(name="three", bufs=3))
         psum = ctx.enter_context(tc.psum_pool(name="psum", bufs=8))
@@ -50,7 +50,7 @@ def tile_bflinear_t_kernel(tc, x_in, weight, bias, grad_out, out):
 
         g_raw = []
         for s in range(GROUPS):
-            g_raw.append(g_pool.tile([P, SUB * K], BF16, name="g_raw"))
+            g_raw.append(per_group.tile([P, SUB * K], BF16, name="g_raw"))
         w_raw = {}
         w_grouped = {}
         w_codes = {}
@@ -67,17 +67,20 @@ def tile_bflinear_t_kernel(tc, x_in, weight, bias, grad_out, out):
         g_codes = {}
         g_scales = {}
         rest_sb = {}
-        out_early = {}
-        out_late = {}
+        out_first = {}
+        out_second = {}
 
-        def load_weight(cols):
-            for c in range(PASSES):
-                for u in range(2):
-                    k0 = c * K_PASS + u * HALF
-                    nc.sync.dma_start(
-                        out=w_raw[cols][:, c, 2 * u : 2 * u + 2, :],
-                        in_=weight[k0 : k0 + HALF, cols[0] : cols[1]].rearrange("(q e) n -> q e n", e=2),
-                    )
+        def load_tokens(s, pair):
+            a, b = 2 * pair * K, (2 * pair + 2) * K
+            nc.sync.dma_start(out=g_raw[s][:, a:b], in_=g_dram[s][:, a:b])
+
+        def load_weight(cols, c):
+            for u in range(2):
+                k0 = c * K_PASS + u * HALF
+                nc.sync.dma_start(
+                    out=w_raw[cols][:, c, 2 * u : 2 * u + 2, :],
+                    in_=weight[k0 : k0 + HALF, cols[0] : cols[1]].rearrange("(q e) n -> q e n", e=2),
+                )
 
         def regroup_weight(c, cols):
             width = cols[1] - cols[0]
@@ -95,17 +98,11 @@ def tile_bflinear_t_kernel(tc, x_in, weight, bias, grad_out, out):
                 in_=w_grouped[cols][:, c, :, :].rearrange("p n t -> p (n t)"),
             )
 
-        def prepare_weight(cols):
-            for c in range(PASSES):
-                regroup_weight(c, cols)
-            for c in range(PASSES):
-                quantise_weight(c, cols)
-
         def transpose_pair(s, pair):
             if pair == 0:
                 g_grouped[s] = two.tile([P, PASSES * GROUP * PACK], BF16, name="g_grouped", align_bytes=64)
-                g_codes[s] = three.tile([P, PASSES, GROUP], U32, name="g_codes", align_bytes=64)
-                g_scales[s] = three.tile([P, PASSES, GROUP], U8, name="g_scales", align_bytes=64)
+                g_codes[s] = per_group.tile([P, PASSES, GROUP], U32, name="g_codes", align_bytes=64)
+                g_scales[s] = per_group.tile([P, PASSES, GROUP], U8, name="g_scales", align_bytes=64)
             words = g_raw[s][:].bitcast(F32).rearrange("p (j w) -> p j w", j=SUB)
             grouped_words = g_grouped[s][:].bitcast(F32).rearrange("p (c r u) -> p c r u", c=PASSES, u=2)
             for c in range(PASSES):
@@ -132,26 +129,34 @@ def tile_bflinear_t_kernel(tc, x_in, weight, bias, grad_out, out):
                 in_=grouped[:, c, r0 * PACK : (r0 + 2 * P) * PACK],
             )
 
+        def window_pass(bank, s, j, cols, c):
+            nc.tensor.matmul_mx(
+                out=bank[:],
+                lhsT=g_codes[s][:, c, j * P : (j + 1) * P].bitcast(E5M2_X4),
+                lhsT_scale=g_scales[s][:, c, j * P : (j + 1) * P],
+                rhs=w_codes[cols][:, c, :].bitcast(E4M3_X4),
+                rhs_scale=w_scales[cols][:, c, :],
+                start=(c == 0),
+                stop=(c == PASSES - 1),
+            )
+
+        def empty_pair(banks, pair, dest):
+            nc.vector.tensor_copy(out=dest[:, 2 * pair, :], in_=banks[0][:])
+            nc.scalar.copy(out=dest[:, 2 * pair + 1, :], in_=banks[1][:])
+
         def window_pair(s, pair, cols, dest):
             banks = [psum.tile([P, N_MOVE], F32, name="bank"), psum.tile([P, N_MOVE], F32, name="bank")]
-            for c in range(PASSES):
-                for jj in range(2):
-                    r0 = (2 * pair + jj) * P
-                    nc.tensor.matmul_mx(
-                        out=banks[jj][:],
-                        lhsT=g_codes[s][:, c, r0 : r0 + P].bitcast(E5M2_X4),
-                        lhsT_scale=g_scales[s][:, c, r0 : r0 + P],
-                        rhs=w_codes[cols][:, c, :].bitcast(E4M3_X4),
-                        rhs_scale=w_scales[cols][:, c, :],
-                        start=(c == 0),
-                        stop=(c == PASSES - 1),
-                    )
-            nc.vector.tensor_copy(out=dest[:, 2 * pair, 0:N_MOVE], in_=banks[0][:])
-            nc.scalar.copy(out=dest[:, 2 * pair + 1, 0:N_MOVE], in_=banks[1][:])
+            for jj in range(2):
+                for c in range(PASSES):
+                    window_pass(banks[jj], s, 2 * pair + jj, cols, c)
+            empty_pair(banks, pair, dest)
 
-        def store_early(s, pair):
+        def store_first(s, pair):
             j0 = 2 * pair
-            nc.sync.dma_start(out=out_dram[s][:, j0 : j0 + 2, FIRST[0] : FIRST[1]], in_=out_early[s][:, j0 : j0 + 2, :])
+            nc.sync.dma_start(out=out_dram[s][:, j0 : j0 + 2, FIRST[0] : FIRST[1]], in_=out_first[s][:, j0 : j0 + 2, :])
+
+        def store_second(s, j):
+            nc.sync.dma_start(out=out_dram[s][:, j, SECOND[0] : SECOND[1]], in_=out_second[s][:, j, :])
 
         def rest_product(s):
             bank = psum.tile([P, N_MOVE], F32, name="bank")
@@ -172,58 +177,77 @@ def tile_bflinear_t_kernel(tc, x_in, weight, bias, grad_out, out):
             bank = psum.tile([P, SUB, P], F32, name="bank")
             for j in range(SUB):
                 nc.tensor.transpose(bank[:, j, :], rest_sb[s][:, j * P : (j + 1) * P], ident[:])
-            nc.vector.tensor_copy(out=out_late[s][:, :, N_MOVE:LATE], in_=bank[:])
+            out_rest = three.tile([P, SUB, P], F32, name="out_rest")
+            nc.vector.tensor_copy(out=out_rest[:], in_=bank[:])
+            nc.sync.dma_start(out=out_dram[s][:, :, REST[0] : REST[1]], in_=out_rest[:])
 
-        nc.sync.dma_start(out=g_raw[0][:, 0 : 2 * K], in_=g_dram[0][:, 0 : 2 * K])
-        load_weight(FIRST)
-        nc.sync.dma_start(out=g_raw[0][:, 2 * K : 4 * K], in_=g_dram[0][:, 2 * K : 4 * K])
-        nc.sync.dma_start(out=g_raw[1][:], in_=g_dram[1])
-        load_weight(REST)
+        load_weight(FIRST, 0)
+        load_tokens(0, 0)
+        load_weight(FIRST, 1)
+        load_tokens(0, 1)
+        load_tokens(1, 0)
+        load_tokens(1, 1)
+        for c in range(PASSES):
+            load_weight(REST, c)
         nc.sync.dma_start(out=g_raw[2][:], in_=g_dram[2])
-        load_weight(SECOND)
+        for c in range(PASSES):
+            load_weight(SECOND, c)
         for s in range(3, GROUPS):
             nc.sync.dma_start(out=g_raw[s][:], in_=g_dram[s])
 
         make_identity(nc, ident[:])
 
+        regroup_weight(0, FIRST)
+        quantise_weight(0, FIRST)
         transpose_pair(0, 0)
-        for c in range(PASSES):
-            regroup_weight(c, FIRST)
-            quantise_pair(0, 0, c)
-            quantise_weight(c, FIRST)
+        quantise_pair(0, 0, 0)
+        regroup_weight(1, FIRST)
+        quantise_pair(0, 0, 1)
+        quantise_weight(1, FIRST)
+        out_first[0] = three.tile([P, SUB, N_MOVE], F32, name="out_first")
+        banks = [psum.tile([P, N_MOVE], F32, name="bank"), psum.tile([P, N_MOVE], F32, name="bank")]
+        for jj in range(2):
+            window_pass(banks[jj], 0, jj, FIRST, 0)
         transpose_pair(0, 1)
+        for jj in range(2):
+            window_pass(banks[jj], 0, jj, FIRST, 1)
+        empty_pair(banks, 0, out_first[0])
         for c in range(PASSES):
             quantise_pair(0, 1, c)
-        prepare_weight(REST)
+        for c in range(PASSES):
+            regroup_weight(c, REST)
+        for c in range(PASSES):
+            quantise_weight(c, REST)
 
-        for s in range(GROUPS + 1):
+        for s in range(GROUPS + LAG):
             now = s < GROUPS
             ahead = s + 1 < GROUPS
-            behind = s >= 1
             if now:
-                out_early[s] = three.tile([P, SUB, N_MOVE], F32, name="out_early")
-                window_pair(s, 0, FIRST, out_early[s])
-                store_early(s, 0)
-            if s == 1:
-                prepare_weight(SECOND)
+                if s > 0:
+                    out_first[s] = three.tile([P, SUB, N_MOVE], F32, name="out_first")
+                    window_pair(s, 0, FIRST, out_first[s])
+                store_first(s, 0)
+            if 1 <= s <= PASSES:
+                regroup_weight(s - 1, SECOND)
+                quantise_weight(s - 1, SECOND)
             if ahead:
                 transpose_pair(s + 1, 0)
                 transpose_pair(s + 1, 1)
                 for c in range(PASSES):
                     quantise_pair(s + 1, 0, c)
-            if behind:
-                out_late[s - 1] = three.tile([P, SUB, LATE], F32, name="out_late")
+            if 1 <= s <= GROUPS:
                 rest_transposes(s - 1)
             if now:
-                window_pair(s, 1, FIRST, out_early[s])
-                store_early(s, 1)
+                window_pair(s, 1, FIRST, out_first[s])
+                store_first(s, 1)
             if ahead:
                 for c in range(PASSES):
                     quantise_pair(s + 1, 1, c)
             if now:
                 rest_product(s)
-            if behind:
+            if s >= LAG:
+                out_second[s - LAG] = three.tile([P, SUB, N_MOVE], F32, name="out_second")
                 for pair in range(PAIRS):
-                    window_pair(s - 1, pair, SECOND, out_late[s - 1])
+                    window_pair(s - LAG, pair, SECOND, out_second[s - LAG])
                     for j in (2 * pair, 2 * pair + 1):
-                        nc.sync.dma_start(out=out_dram[s - 1][:, j, SECOND[0] : REST[1]], in_=out_late[s - 1][:, j, :])
+                        store_second(s - LAG, j)

from contextlib import ExitStack

import concourse.mybir as mybir
from concourse.masks import make_identity

BF16 = mybir.dt.bfloat16
F32 = mybir.dt.float32
U32 = mybir.dt.uint32
U8 = mybir.dt.uint8
E4M3_X4 = mybir.dt.float8_e4m3fn_x4
E5M2_X4 = mybir.dt.float8_e5m2_x4

TOKENS = 3072
K = 1024
COLS = 1152

P = 128
PACK = 4
K_PASS = P * PACK
PASSES = K // K_PASS
HALF = K_PASS // 2
N_MOVE = 512

SUB = 4
PAIRS = SUB // 2
GROUP = P * SUB
GROUPS = TOKENS // GROUP

FIRST = (0, N_MOVE)
SECOND = (N_MOVE, 2 * N_MOVE)
REST = (2 * N_MOVE, COLS)
LAG = 2

FLOPS = 2 * TOKENS * K * COLS
BYTES = TOKENS * K * 2 + K * COLS * 2 + TOKENS * COLS * 4


def tile_bflinear_t_kernel(tc, x_in, weight, bias, grad_out, out):
    nc = tc.nc
    g_dram = grad_out.rearrange("(s p j) k -> s p (j k)", p=P, j=SUB)
    out_dram = out.rearrange("(s p j) n -> s p j n", p=P, j=SUB)

    with ExitStack() as ctx:
        keep = ctx.enter_context(tc.tile_pool(name="keep", bufs=1))
        per_group = ctx.enter_context(tc.tile_pool(name="per_group", bufs=GROUPS))
        two = ctx.enter_context(tc.tile_pool(name="two", bufs=2))
        three = ctx.enter_context(tc.tile_pool(name="three", bufs=3))
        psum = ctx.enter_context(tc.psum_pool(name="psum", bufs=8))
        ctx.enter_context(tc.manual_schedule())

        g_raw = []
        for s in range(GROUPS):
            g_raw.append(per_group.tile([P, SUB * K], BF16, name="g_raw"))
        w_raw = {}
        w_grouped = {}
        w_codes = {}
        w_scales = {}
        for cols in (FIRST, SECOND, REST):
            width = cols[1] - cols[0]
            w_raw[cols] = keep.tile([P, PASSES, PACK, width], BF16, name="w_raw%d" % cols[0])
            w_grouped[cols] = keep.tile([P, PASSES, width, PACK], BF16, name="w_grouped%d" % cols[0], align_bytes=64)
            w_codes[cols] = keep.tile([P, PASSES, width], U32, name="w_codes%d" % cols[0], align_bytes=64)
            w_scales[cols] = keep.tile([P, PASSES, width], U8, name="w_scales%d" % cols[0], align_bytes=64)
        ident = keep.tile([P, P], F32)

        g_grouped = {}
        g_codes = {}
        g_scales = {}
        rest_sb = {}
        out_first = {}
        out_second = {}

        def load_tokens(s, pair):
            a, b = 2 * pair * K, (2 * pair + 2) * K
            nc.sync.dma_start(out=g_raw[s][:, a:b], in_=g_dram[s][:, a:b])

        def load_weight(cols, c):
            for u in range(2):
                k0 = c * K_PASS + u * HALF
                nc.sync.dma_start(
                    out=w_raw[cols][:, c, 2 * u : 2 * u + 2, :],
                    in_=weight[k0 : k0 + HALF, cols[0] : cols[1]].rearrange("(q e) n -> q e n", e=2),
                )

        def regroup_weight(c, cols):
            width = cols[1] - cols[0]
            cut = width * 5 // 8
            for engine_copy, a, b in ((nc.vector.tensor_copy, 0, cut), (nc.scalar.copy, cut, width)):
                engine_copy(
                    out=w_grouped[cols][:, c, a:b, :].rearrange("p (n i) t -> p n t i", i=4),
                    in_=w_raw[cols][:, c, :, a:b].rearrange("p t (n i) -> p n t i", i=4),
                )

        def quantise_weight(c, cols):
            nc.vector.quantize_mx(
                out=w_codes[cols][:, c, :].bitcast(E4M3_X4),
                scales=w_scales[cols][:, c, :],
                in_=w_grouped[cols][:, c, :, :].rearrange("p n t -> p (n t)"),
            )

        def transpose_pair(s, pair):
            if pair == 0:
                g_grouped[s] = two.tile([P, PASSES * GROUP * PACK], BF16, name="g_grouped", align_bytes=64)
                g_codes[s] = per_group.tile([P, PASSES, GROUP], U32, name="g_codes", align_bytes=64)
                g_scales[s] = per_group.tile([P, PASSES, GROUP], U8, name="g_scales", align_bytes=64)
            words = g_raw[s][:].bitcast(F32).rearrange("p (j w) -> p j w", j=SUB)
            grouped_words = g_grouped[s][:].bitcast(F32).rearrange("p (c r u) -> p c r u", c=PASSES, u=2)
            for c in range(PASSES):
                bank = psum.tile([P, 2, 2 * P], F32, name="bank")
                for u in range(2):
                    for jj in range(2):
                        w0 = (c * K_PASS + u * HALF) // 2
                        nc.tensor.transpose(
                            bank[:, u, jj * P : (jj + 1) * P],
                            words[:, 2 * pair + jj, w0 : w0 + P],
                            ident[:],
                        )
                nc.scalar.copy(
                    out=grouped_words[:, c, 2 * pair * P : (2 * pair + 2) * P, :],
                    in_=bank[:].rearrange("p u r -> p r u"),
                )

        def quantise_pair(s, pair, c):
            grouped = g_grouped[s][:].rearrange("p (c x) -> p c x", c=PASSES)
            r0 = 2 * pair * P
            nc.vector.quantize_mx(
                out=g_codes[s][:, c, r0 : r0 + 2 * P].bitcast(E5M2_X4),
                scales=g_scales[s][:, c, r0 : r0 + 2 * P],
                in_=grouped[:, c, r0 * PACK : (r0 + 2 * P) * PACK],
            )

        def window_pass(bank, s, j, cols, c):
            nc.tensor.matmul_mx(
                out=bank[:],
                lhsT=g_codes[s][:, c, j * P : (j + 1) * P].bitcast(E5M2_X4),
                lhsT_scale=g_scales[s][:, c, j * P : (j + 1) * P],
                rhs=w_codes[cols][:, c, :].bitcast(E4M3_X4),
                rhs_scale=w_scales[cols][:, c, :],
                start=(c == 0),
                stop=(c == PASSES - 1),
            )

        def empty_pair(banks, pair, dest):
            nc.vector.tensor_copy(out=dest[:, 2 * pair, :], in_=banks[0][:])
            nc.scalar.copy(out=dest[:, 2 * pair + 1, :], in_=banks[1][:])

        def window_pair(s, pair, cols, dest):
            banks = [psum.tile([P, N_MOVE], F32, name="bank"), psum.tile([P, N_MOVE], F32, name="bank")]
            for jj in range(2):
                for c in range(PASSES):
                    window_pass(banks[jj], s, 2 * pair + jj, cols, c)
            empty_pair(banks, pair, dest)

        def store_first(s, pair):
            j0 = 2 * pair
            nc.sync.dma_start(out=out_dram[s][:, j0 : j0 + 2, FIRST[0] : FIRST[1]], in_=out_first[s][:, j0 : j0 + 2, :])

        def store_second(s, j):
            nc.sync.dma_start(out=out_dram[s][:, j, SECOND[0] : SECOND[1]], in_=out_second[s][:, j, :])

        def rest_product(s):
            bank = psum.tile([P, N_MOVE], F32, name="bank")
            for c in range(PASSES):
                nc.tensor.matmul_mx(
                    out=bank[:],
                    lhsT=w_codes[REST][:, c, :].bitcast(E4M3_X4),
                    lhsT_scale=w_scales[REST][:, c, :],
                    rhs=g_codes[s][:, c, :].bitcast(E5M2_X4),
                    rhs_scale=g_scales[s][:, c, :],
                    start=(c == 0),
                    stop=(c == PASSES - 1),
                )
            rest_sb[s] = two.tile([P, GROUP], F32, name="rest_sb")
            nc.scalar.copy(out=rest_sb[s][:], in_=bank[:])

        def rest_transposes(s):
            bank = psum.tile([P, SUB, P], F32, name="bank")
            for j in range(SUB):
                nc.tensor.transpose(bank[:, j, :], rest_sb[s][:, j * P : (j + 1) * P], ident[:])
            out_rest = three.tile([P, SUB, P], F32, name="out_rest")
            nc.vector.tensor_copy(out=out_rest[:], in_=bank[:])
            nc.sync.dma_start(out=out_dram[s][:, :, REST[0] : REST[1]], in_=out_rest[:])

        load_weight(FIRST, 0)
        load_tokens(0, 0)
        load_weight(FIRST, 1)
        load_tokens(0, 1)
        load_tokens(1, 0)
        load_tokens(1, 1)
        for c in range(PASSES):
            load_weight(REST, c)
        nc.sync.dma_start(out=g_raw[2][:], in_=g_dram[2])
        for c in range(PASSES):
            load_weight(SECOND, c)
        for s in range(3, GROUPS):
            nc.sync.dma_start(out=g_raw[s][:], in_=g_dram[s])

        make_identity(nc, ident[:])

        regroup_weight(0, FIRST)
        quantise_weight(0, FIRST)
        transpose_pair(0, 0)
        quantise_pair(0, 0, 0)
        regroup_weight(1, FIRST)
        quantise_pair(0, 0, 1)
        quantise_weight(1, FIRST)
        out_first[0] = three.tile([P, SUB, N_MOVE], F32, name="out_first")
        banks = [psum.tile([P, N_MOVE], F32, name="bank"), psum.tile([P, N_MOVE], F32, name="bank")]
        for jj in range(2):
            window_pass(banks[jj], 0, jj, FIRST, 0)
        transpose_pair(0, 1)
        for jj in range(2):
            window_pass(banks[jj], 0, jj, FIRST, 1)
        empty_pair(banks, 0, out_first[0])
        for c in range(PASSES):
            quantise_pair(0, 1, c)
        for c in range(PASSES):
            regroup_weight(c, REST)
        for c in range(PASSES):
            quantise_weight(c, REST)

        for s in range(GROUPS + LAG):
            now = s < GROUPS
            ahead = s + 1 < GROUPS
            if now:
                if s > 0:
                    out_first[s] = three.tile([P, SUB, N_MOVE], F32, name="out_first")
                    window_pair(s, 0, FIRST, out_first[s])
                store_first(s, 0)
            if 1 <= s <= PASSES:
                regroup_weight(s - 1, SECOND)
                quantise_weight(s - 1, SECOND)
            if ahead:
                transpose_pair(s + 1, 0)
                transpose_pair(s + 1, 1)
                for c in range(PASSES):
                    quantise_pair(s + 1, 0, c)
            if 1 <= s <= GROUPS:
                rest_transposes(s - 1)
            if now:
                window_pair(s, 1, FIRST, out_first[s])
                store_first(s, 1)
            if ahead:
                for c in range(PASSES):
                    quantise_pair(s + 1, 1, c)
            if now:
                rest_product(s)
            if s >= LAG:
                out_second[s - LAG] = three.tile([P, SUB, N_MOVE], F32, name="out_second")
                for pair in range(PAIRS):
                    window_pair(s - LAG, pair, SECOND, out_second[s - LAG])
                    for j in (2 * pair, 2 * pair + 1):
                        store_second(s - LAG, j)
